import numpy as np
import ml_dtypes


def mxq(x, axis, fmt="e4m3"):
    dtype, down = {"e4m3": (ml_dtypes.float8_e4m3fn, 7), "e5m2": (ml_dtypes.float8_e5m2, 14)}[fmt]
    v = np.moveaxis(np.asarray(x, np.float32).astype(ml_dtypes.bfloat16).astype(np.float64), axis, -1)
    blocks = v.reshape(v.shape[:-1] + (-1, 32))
    amax = np.abs(blocks).max(-1, keepdims=True)
    byte = np.maximum(np.where(amax > 0, np.frexp(amax)[1] - 1 + 127, 0) - down, 1)
    scale = np.exp2(byte - 127.0)
    codes = (blocks / scale).astype(np.float32).astype(dtype).astype(np.float64)
    return np.moveaxis((codes * scale).reshape(v.shape), -1, axis)


WIDE = False


def mx_kscale(k):
    if not WIDE:
        return np.ones(k)
    levels = np.array([10, -10, 5, -5, 0])
    if k % 512:
        return np.exp2(np.random.permutation(np.resize(levels, k // 32))).repeat(32)
    a = np.empty((k // 512, 16))
    for p in range(k // 512):
        a[p, :8] = np.random.permutation(np.resize(levels, 8))
        for g in range(8):
            far = levels[np.abs(levels - a[p, g]) >= 10]
            a[p, g + 8] = far[np.random.randint(len(far))]
    return np.exp2(a.ravel()).repeat(32)


BF16 = ml_dtypes.bfloat16


def bf(x):
    return np.asarray(x, np.float32).astype(BF16)


def f64(x):
    return np.asarray(x).astype(np.float64)


H, A, NS, NE, M = 2048, 2048, 4096, 2048, 2048


def setup_inputs():
    s, t = mx_kscale(H), mx_kscale(H)
    wsc = 0.25 / np.sqrt(H)
    return {
        "attendee_stmts": bf(np.random.standard_normal((NS, H)) * s),
        "attendee_eres": bf(np.random.standard_normal((NE, H)) * s),
        "attender": bf(np.random.standard_normal((M, H)) * 0.2 / t),
        "W_ss": bf(np.random.standard_normal((H, H)) * wsc * t[:, None] / s),
        "b_ss": bf(np.random.standard_normal(H) * 0.1 * t),
        "W_es": bf(np.random.standard_normal((H, H)) * wsc * t[:, None] / s),
        "b_es": bf(np.random.standard_normal(H) * 0.1 * t),
    }


def reference(attendee_stmts, attendee_eres, attender, W_ss, b_ss, W_es, b_es):
    aq = mxq(f64(attender), 1, "e4m3")
    p_ss = (mxq(f64(attendee_stmts), 1, "e4m3") @ mxq(f64(W_ss), 1, "e4m3").T) + f64(b_ss)
    p_es = (mxq(f64(attendee_eres), 1, "e4m3") @ mxq(f64(W_es), 1, "e4m3").T) + f64(b_es)
    scores_ss = mxq(p_ss, 1, "e4m3") @ aq.T
    scores_es = mxq(p_es, 1, "e4m3") @ aq.T
    return scores_ss, scores_es

@@ -1,0 +1,314 @@
+from contextlib import ExitStack
+
+import concourse.mybir as mybir
+from concourse.masks import make_identity
+
+F32 = mybir.dt.float32
+BF16 = mybir.dt.bfloat16
+U32 = mybir.dt.uint32
+U8 = mybir.dt.uint8
+FP8X4 = mybir.dt.float8_e4m3fn_x4
+IDENT = mybir.ActivationFunctionType.Identity
+
+P = 128
+NCH = 12
+LAG = 5
+NSTEP = 4 * NCH + LAG
+WES0 = 12
+NRAWH = 6
+FLOPS = 2 * 2 * (4096 + 2048) * 2048 * 2048
+
+
+def tile_attention_pa_l_kernel(tc, attendee_stmts, attendee_eres, attender, W_ss, b_ss, W_es, b_es, out_0, out_1):
+    nc = tc.nc
+    with ExitStack() as ctx:
+        sb = ctx.enter_context(tc.tile_pool(name="sb", bufs=1))
+        psum = ctx.enter_context(tc.psum_pool(name="psum", bufs=4))
+
+        def sbt(shape, dtype, tag, bufs):
+            return sb.tile(shape, dtype, name=tag, tag=tag, bufs=bufs, align_bytes=64)
+
+        def chunk_src(c):
+            if c < 8:
+                return attendee_stmts, 512 * c, 0, out_0
+            return attendee_eres, 512 * (c - 8), 1, out_1
+
+        ident = sbt([P, P], F32, "ident", 1)
+        make_identity(nc, ident[:])
+        warm = sbt([P, 1], F32, "warm", 1)
+        warm2 = sbt([P, 1], F32, "warm2", 1)
+        nc.vector.memset(warm[:], 0.0)
+        nc.scalar.activation(out=warm2[:], in_=warm[:], func=IDENT)
+        bias = []
+        for mat, b in enumerate((b_ss, b_es)):
+            braw = sbt([P, 16], BF16, "braw%d" % mat, 1)
+            nc.scalar.dma_start(out=braw[:].rearrange("c (G t) -> c G t", t=4), in_=b.rearrange("(G c t) -> c G t", G=4, c=P, t=4))
+            bf = sbt([P, 16], F32, "bias%d" % mat, 1)
+            nc.vector.tensor_copy(out=bf[:], in_=braw[:])
+            bias.append(bf)
+
+        ctx.enter_context(tc.manual_schedule())
+
+        xq, pq, psc, wq, aq, asc = {}, {}, {}, {}, {}, {}
+
+        def get_x(c):
+            if c not in xq:
+                codes = []
+                for g in range(4):
+                    codes.append(sbt([P, 512], U32, "xq%d" % g, 2))
+                xq[c] = (codes, sbt([P, 512], U8, "xsc", 2))
+            return xq[c]
+
+        def get_w(mat, G, t):
+            if (mat, G, t) not in wq:
+                sc = sbt([P, P], U8, "ws%d_%d_%d" % (mat, G, t), 1)
+                if mat == 0:
+                    wq[(mat, G, t)] = (sbt([P, 512], U32, "wq0_%d_%d" % (G, t), 1), sc)
+                else:
+                    if t % 2 == 0:
+                        both = sbt([P, 1024], U32, "ovl", 8)
+                        wq[(mat, G, t)] = (both[:, 0:512], sc)
+                        wq[(mat, G, t + 1, "codes")] = both[:, 512:1024]
+                    else:
+                        wq[(mat, G, t)] = (wq[(mat, G, t, "codes")], sc)
+            return wq[(mat, G, t)]
+
+        def get_a(G, ar):
+            if (G, ar) not in aq:
+                aq[(G, ar)] = sbt([P, 512], U32, "aq%d_%d" % (G, ar), 1)
+            if ar not in asc:
+                asc[ar] = sbt([P, 512], U8, "asc%d" % ar, 1)
+            return aq[(G, ar)], asc[ar]
+
+        def dest(d, g):
+            if d[0] == "x":
+                codes, sc = get_x(d[1])
+                lo = P * d[2]
+                return codes[g][:, lo:lo + P], sc[4 * g:P, lo:lo + P]
+            if d[0] == "w":
+                codes, sc = get_w(d[1], d[2], d[3])
+                return codes[:, P * g:P * g + P], sc[4 * g:P, :]
+            codes, sc = get_a(g, d[1] // 4)
+            lo = P * (d[1] % 4)
+            return codes[:, lo:lo + P], sc[4 * g:P, lo:lo + P]
+
+        def quantize(job):
+            for g in range(4):
+                codes, sc = dest(job["dest"], g)
+                nc.vector.quantize_mx(out=codes.bitcast(FP8X4), scales=sc, in_=job["grp"][:, 512 * g:512 * g + 512])
+
+        pe_jobs = []
+        for rt in range(4):
+            pe_jobs.append({"kind": "P1", "rows": attendee_stmts[P * rt:P * rt + P, :], "dest": ("x", 0, rt)})
+        wss_view = W_ss.rearrange("(G c t) k -> G t c k", G=4, c=P, t=4)
+        for G in range(4):
+            for t in range(4):
+                pe_jobs.append({"kind": "P1", "rows": wss_view[G, t], "dest": ("w", 0, G, t)})
+        for at in range(16):
+            pe_jobs.append({"kind": "P2", "rows": attender[P * at:P * at + P, :], "dest": ("a", at)})
+        by_sig = {}
+        for n, job in enumerate(pe_jobs):
+            sg = n - 8 if n < 8 else (n - 8) // 2
+            by_sig[sg] = by_sig.get(sg, []) + [job]
+
+        wes_view = W_es.rearrange("(G rb j t) k -> G t j rb k", G=4, rb=4, j=32, t=4)
+        wjobs = {}
+        for w in range(16):
+            wjobs[WES0 + w] = {"kind": "V", "dest": ("w", 1, w // 4, w % 4), "wsrc": wes_view[w // 4, w % 4]}
+        xjobs = {}
+        for v in range(44):
+            xjobs[v] = {"kind": "V", "dest": ("x", 1 + v // 4, v % 4), "pair": v // 2, "half": v % 2}
+
+        def quad_load(raw, src, a):
+            eng = nc.sync if a < 2 else nc.scalar
+            eng.dma_start(out=raw[32 * a:32 * a + 32, :].rearrange("p (rb k) -> p rb k", k=512), in_=src[:, :, 512 * a:512 * a + 512])
+
+        hqueue = pe_jobs + [wjobs[WES0 + w] for w in range(16)]
+        hstate = {"next": 0}
+
+        def load_next_h():
+            n = hstate["next"]
+            if n >= len(hqueue):
+                return
+            hstate["next"] = n + 1
+            job = hqueue[n]
+            raw = sbt([P, 2048], BF16, "rawh", NRAWH)
+            if job["kind"] == "V":
+                for a in range(4):
+                    quad_load(raw, job["wsrc"], a)
+            else:
+                nc.sync.dma_start(out=raw[:], in_=job["rows"])
+            job["words"] = raw[:].bitcast(F32)
+
+        def load_pair(n):
+            if n >= 22:
+                return
+            X, r0, mat, out = chunk_src(1 + n // 2)
+            r0 = r0 + 256 * (n % 2)
+            raw = sbt([P, 4096], BF16, "rawx", 3)
+            src = X[r0:r0 + 256, :].rearrange("(rb j) k -> j rb k", j=32)
+            for a in range(4):
+                quad_load(raw, src, a)
+            words = raw[:].bitcast(F32)
+            xjobs[2 * n]["words"] = words[:, 0:1024]
+            xjobs[2 * n + 1]["words"] = words[:, 1024:2048]
+
+        def pe_sort(job):
+            if job["kind"] == "P1":
+                srt = sbt([P, 1024], F32, "ovl", 8)
+                for u in range(2):
+                    nc.vector.tensor_copy(
+                        out=srt[:].rearrange("p (g u a i) -> p u g a i", g=4, u=2, a=4, i=32)[:, u],
+                        in_=job["words"].rearrange("p (a g i u) -> p u g a i", a=4, g=4, i=32, u=2)[:, u],
+                    )
+                job["srt"] = srt
+                load_next_h()
+
+        def pe_transposes(job):
+            job["banks"] = []
+            for hb in range(2):
+                bank = psum.tile([P, 512], F32, name="tp", tag="m2")
+                for sl in range(4):
+                    idx = 4 * hb + sl
+                    if job["kind"] == "P1":
+                        src = job["srt"][:, P * idx:P * idx + P]
+                    else:
+                        src = job["words"][:, 256 * (idx // 2) + idx % 2:256 * (idx // 2) + 256:2]
+                    nc.tensor.transpose(out=bank[:, P * sl:P * sl + P], in_=src, identity=ident[:])
+                job["banks"].append(bank)
+            if job["kind"] == "P2":
+                load_next_h()
+
+        def pe_copy(job):
+            grp = sbt([P, 2048], BF16, "ovl", 8)
+            for hb in range(2):
+                nc.scalar.copy(
+                    out=grp[:].bitcast(F32)[:, 512 * hb:512 * hb + 512].rearrange("p (g r u) -> p g r u", g=2, r=P, u=2),
+                    in_=job["banks"][hb][:].rearrange("p (g u r) -> p g r u", g=2, u=2, r=P),
+                )
+            job["grp"] = grp
+
+        def v_sort(job, u):
+            if u == 0:
+                job["srt"] = sbt([P, 1024], F32, "srtv", 3)
+            nc.scalar.copy(
+                out=job["srt"][:].rearrange("p (g rb u i) -> p u g rb i", g=4, rb=4, u=2, i=32)[:, u],
+                in_=job["words"].rearrange("p (rb g i u) -> p u g rb i", rb=4, g=4, i=32, u=2)[:, u],
+            )
+
+        def v_tr(job):
+            job["trn"] = sbt([P, 1024], F32, "trn", 1)
+            nc.vector.transpose(out=job["trn"][:], in_=job["srt"][:])
+
+        def v_il(job):
+            job["grp"] = sbt([P, 2048], BF16, "grp", 2)
+            nc.vector.tensor_copy(
+                out=job["grp"][:].bitcast(F32).rearrange("p (x j u) -> p x j u", x=16, j=32, u=2),
+                in_=job["trn"][:].rearrange("p (x u j) -> p x j u", x=16, u=2, j=32),
+            )
+
+        acc1, acc2, pTs, pGs = {}, {}, {}, {}
+
+        def m1(s, t):
+            c, G = divmod(s, 4)
+            mat = chunk_src(c)[2]
+            codes, sc = get_x(c)
+            wc, wsc = get_w(mat, G, t)
+            acc = psum.tile([P, 512], F32, name="m1", tag="m1")
+            for g in range(4):
+                nc.tensor.matmul_mx(
+                    out=acc[:], lhsT=wc[:, P * g:P * g + P].bitcast(FP8X4), lhsT_scale=wsc[4 * g:P, :],
+                    rhs=codes[g][:].bitcast(FP8X4), rhs_scale=sc[4 * g:P, :], start=(g == 0), stop=(g == 3),
+                )
+            acc1[(s, t)] = acc
+
+        def e1(s, t):
+            c, G = divmod(s, 4)
+            mat = chunk_src(c)[2]
+            if t == 0:
+                pTs[s] = sbt([P, 4, 512], BF16, "pT", 2)
+            nc.scalar.activation(out=pTs[s][:, t, :], in_=acc1[(s, t)][:], func=IDENT, bias=bias[mat][:, 4 * G + t:4 * G + t + 1])
+
+        def p_interleave(s):
+            pGs[s] = sbt([P, 2048], BF16, "pG", 1)
+            nc.vector.tensor_copy(out=pGs[s][:].rearrange("p (n t) -> p n t", t=4), in_=pTs[s][:].rearrange("p t n -> p n t"))
+
+        def p_quantize(s):
+            c, G = divmod(s, 4)
+            if G == 0:
+                psc[c] = sbt([P, 512], U8, "psc", 2)
+            pq[(c, G)] = sbt([P, 512], U32, "pq%d" % G, 2)
+            nc.vector.quantize_mx(out=pq[(c, G)][:].bitcast(FP8X4), scales=psc[c][4 * G:P, :], in_=pGs[s][:])
+
+        def m2(s, ar):
+            c, tt = divmod(s, 4)
+            acc = psum.tile([P, 512], F32, name="m2", tag="m2")
+            for G in range(4):
+                ac, asl = get_a(G, ar)
+                nc.tensor.matmul_mx(
+                    out=acc[:], lhsT=pq[(c, G)][:, P * tt:P * tt + P].bitcast(FP8X4), lhsT_scale=psc[c][4 * G:P, P * tt:P * tt + P],
+                    rhs=ac[:].bitcast(FP8X4), rhs_scale=asl[4 * G:P, :], start=(G == 0), stop=(G == 3),
+                )
+            acc2[(s, ar)] = acc
+
+        def e2(s, ar):
+            c, tt = divmod(s, 4)
+            X, r0, mat, out = chunk_src(c)
+            ob = sbt([P, 512], F32, "ob", 4)
+            nc.scalar.copy(out=ob[:], in_=acc2[(s, ar)][:])
+            nc.sync.dma_start(out=out[r0 + P * tt:r0 + P * tt + P, 512 * ar:512 * ar + 512], in_=ob[:])
+
+        for n in range(NRAWH):
+            load_next_h()
+        load_pair(0)
+
+        for sig in range(-8, 4 * NSTEP):
+            s, j = divmod(sig, 4)
+            if sig == -2:
+                load_pair(1)
+            if sig == 4:
+                load_pair(2)
+            for job in by_sig.get(sig, []):
+                pe_sort(job)
+            for job in by_sig.get(sig - 2, []):
+                quantize(job)
+            for job in by_sig.get(sig - 1, []):
+                pe_transposes(job)
+            for job in by_sig.get(sig - 1, []):
+                pe_copy(job)
+            if 0 <= s < 48:
+                m1(s, j)
+            if 0 <= s - LAG < 48:
+                m2(s - LAG, j)
+            if 0 <= s < 48:
+                e1(s, j)
+            if 0 <= s - LAG < 48:
+                e2(s - LAG, j)
+            xj, wj = xjobs.get(s), wjobs.get(s)
+            if j == 0:
+                if xj:
+                    v_tr(xj)
+                if 0 <= s - 1 < 48:
+                    p_interleave(s - 1)
+            if j == 1:
+                if xj:
+                    v_il(xj)
+                if 0 <= s - 1 < 48:
+                    p_quantize(s - 1)
+            if j == 2:
+                if wj:
+                    v_tr(wj)
+                if xj:
+                    quantize(xj)
+            if j == 3 and wj:
+                v_il(wj)
+                quantize(wj)
+            xn, wn = xjobs.get(s + 1), wjobs.get(s + 1)
+            if j < 2 and xn:
+                v_sort(xn, j)
+            if j >= 2 and wn:
+                v_sort(wn, j - 2)
+                if j == 3:
+                    load_next_h()
+            if j == 2 and s >= 0 and s % 2 == 0:
+                load_pair(s // 2 + 3)

@@ -16,6 +16,8 @@ LAG = 5
 NSTEP = 4 * NCH + LAG
 WES0 = 12
 NRAWH = 6
+A_KINDS = ("P2", "P2")
+XLOADS = (1, 3, 6, 12, 16)
 FLOPS = 2 * 2 * (4096 + 2048) * 2048 * 2048
 
 
@@ -25,8 +27,8 @@ def tile_attention_pa_l_kernel(tc, attendee_stmts, attendee_eres, attender, W_ss
         sb = ctx.enter_context(tc.tile_pool(name="sb", bufs=1))
         psum = ctx.enter_context(tc.psum_pool(name="psum", bufs=4))
 
-        def sbt(shape, dtype, tag, bufs):
-            return sb.tile(shape, dtype, name=tag, tag=tag, bufs=bufs, align_bytes=64)
+        def sbt(shape, dtype, tag, bufs, align=64):
+            return sb.tile(shape, dtype, name=tag, tag=tag, bufs=bufs, align_bytes=align)
 
         def chunk_src(c):
             if c < 8:
@@ -49,42 +51,37 @@ def tile_attention_pa_l_kernel(tc, attendee_stmts, attendee_eres, attender, W_ss
 
         ctx.enter_context(tc.manual_schedule())
 
-        xq, pq, psc, wq, aq, asc = {}, {}, {}, {}, {}, {}
+        xq, pq, psc, wq, aq = {}, {}, {}, {}, {}
 
         def get_x(c):
             if c not in xq:
-                codes = []
-                for g in range(4):
-                    codes.append(sbt([P, 512], U32, "xq%d" % g, 2))
-                xq[c] = (codes, sbt([P, 512], U8, "xsc", 2))
+                xq[c] = (sbt([P, 2048], U32, "xq", 2, 256), sbt([P, 512], U8, "xsc", 2, 256))
             return xq[c]
 
+        wsc = [sbt([P, 16 * 256], U8, "ws0", 1, 256), sbt([P, 16 * 256], U8, "ws1", 1, 256)]
+
         def get_w(mat, G, t):
-            if (mat, G, t) not in wq:
-                sc = sbt([P, P], U8, "ws%d_%d_%d" % (mat, G, t), 1)
-                if mat == 0:
-                    wq[(mat, G, t)] = (sbt([P, 512], U32, "wq0_%d_%d" % (G, t), 1), sc)
-                else:
-                    if t % 2 == 0:
-                        both = sbt([P, 1024], U32, "ovl", 8)
-                        wq[(mat, G, t)] = (both[:, 0:512], sc)
-                        wq[(mat, G, t + 1, "codes")] = both[:, 512:1024]
-                    else:
-                        wq[(mat, G, t)] = (wq[(mat, G, t, "codes")], sc)
-            return wq[(mat, G, t)]
+            sc = wsc[mat][:, 256 * (4 * G + t):256 * (4 * G + t) + P]
+            if mat == 0:
+                if (mat, G) not in wq:
+                    wq[(mat, G)] = sbt([P, 2048], U32, "wq0_%d" % G, 1, 256)
+                return wq[(mat, G)][:, 512 * t:512 * t + 512], sc
+            if (mat, G, t // 2) not in wq:
+                wq[(mat, G, t // 2)] = sbt([P, 1024], U32, "ovl", 8, 256)
+            return wq[(mat, G, t // 2)][:, 512 * (t % 2):512 * (t % 2) + 512], sc
+
+        asc = sbt([P, 2048], U8, "asc", 1, 256)
 
         def get_a(G, ar):
-            if (G, ar) not in aq:
-                aq[(G, ar)] = sbt([P, 512], U32, "aq%d_%d" % (G, ar), 1)
-            if ar not in asc:
-                asc[ar] = sbt([P, 512], U8, "asc%d" % ar, 1)
-            return aq[(G, ar)], asc[ar]
+            if ar not in aq:
+                aq[ar] = sbt([P, 2048], U32, "aq%d" % ar, 1, 256)
+            return aq[ar][:, 512 * G:512 * G + 512], asc[:, 512 * ar:512 * ar + 512]
 
         def dest(d, g):
             if d[0] == "x":
                 codes, sc = get_x(d[1])
                 lo = P * d[2]
-                return codes[g][:, lo:lo + P], sc[4 * g:P, lo:lo + P]
+                return codes[:, 512 * g + lo:512 * g + lo + P], sc[4 * g:P, lo:lo + P]
             if d[0] == "w":
                 codes, sc = get_w(d[1], d[2], d[3])
                 return codes[:, P * g:P * g + P], sc[4 * g:P, :]
@@ -97,15 +94,17 @@ def tile_attention_pa_l_kernel(tc, attendee_stmts, attendee_eres, attender, W_ss
                 codes, sc = dest(job["dest"], g)
                 nc.vector.quantize_mx(out=codes.bitcast(FP8X4), scales=sc, in_=job["grp"][:, 512 * g:512 * g + 512])
 
-        pe_jobs = []
+        x0_jobs, x1_jobs, w_jobs, a_jobs = [], [], [], []
         for rt in range(4):
-            pe_jobs.append({"kind": "P1", "rows": attendee_stmts[P * rt:P * rt + P, :], "dest": ("x", 0, rt)})
+            x0_jobs.append({"kind": "P1", "dest": ("x", 0, rt), "last": rt % 2 == 1})
+            x1_jobs.append({"kind": "P1", "dest": ("x", 1, rt), "last": rt % 2 == 1})
         wss_view = W_ss.rearrange("(G c t) k -> G t c k", G=4, c=P, t=4)
         for G in range(4):
             for t in range(4):
-                pe_jobs.append({"kind": "P1", "rows": wss_view[G, t], "dest": ("w", 0, G, t)})
+                w_jobs.append({"kind": "P1", "rows": wss_view[G, t], "dest": ("w", 0, G, t)})
         for at in range(16):
-            pe_jobs.append({"kind": "P2", "rows": attender[P * at:P * at + P, :], "dest": ("a", at)})
+            a_jobs.append({"kind": A_KINDS[at % 2], "rows": attender[P * at:P * at + P, :], "dest": ("a", at)})
+        pe_jobs = x0_jobs + w_jobs + x1_jobs + a_jobs
         by_sig = {}
         for n, job in enumerate(pe_jobs):
             sg = n - 8 if n < 8 else (n - 8) // 2
@@ -116,14 +115,14 @@ def tile_attention_pa_l_kernel(tc, attendee_stmts, attendee_eres, attender, W_ss
         for w in range(16):
             wjobs[WES0 + w] = {"kind": "V", "dest": ("w", 1, w // 4, w % 4), "wsrc": wes_view[w // 4, w % 4]}
         xjobs = {}
-        for v in range(44):
+        for v in range(4, 44):
             xjobs[v] = {"kind": "V", "dest": ("x", 1 + v // 4, v % 4), "pair": v // 2, "half": v % 2}
 
         def quad_load(raw, src, a):
             eng = nc.sync if a < 2 else nc.scalar
             eng.dma_start(out=raw[32 * a:32 * a + 32, :].rearrange("p (rb k) -> p rb k", k=512), in_=src[:, :, 512 * a:512 * a + 512])
 
-        hqueue = pe_jobs + [wjobs[WES0 + w] for w in range(16)]
+        hqueue = w_jobs + a_jobs + [wjobs[WES0 + w] for w in range(16)]
         hstate = {"next": 0}
 
         def load_next_h():
@@ -140,29 +139,49 @@ def tile_attention_pa_l_kernel(tc, attendee_stmts, attendee_eres, attender, W_ss
                 nc.sync.dma_start(out=raw[:], in_=job["rows"])
             job["words"] = raw[:].bitcast(F32)
 
-        def load_pair(n):
-            if n >= 22:
+        xstate = {"next": 0}
+
+        def load_next_x():
+            n = xstate["next"]
+            if n >= 24:
                 return
-            X, r0, mat, out = chunk_src(1 + n // 2)
+            xstate["next"] = n + 1
+            X, r0, mat, out = chunk_src(n // 2)
             r0 = r0 + 256 * (n % 2)
             raw = sbt([P, 4096], BF16, "rawx", 3)
-            src = X[r0:r0 + 256, :].rearrange("(rb j) k -> j rb k", j=32)
-            for a in range(4):
-                quad_load(raw, src, a)
             words = raw[:].bitcast(F32)
-            xjobs[2 * n]["words"] = words[:, 0:1024]
-            xjobs[2 * n + 1]["words"] = words[:, 1024:2048]
+            if n < 4:
+                for h in range(2):
+                    nc.sync.dma_start(out=raw[:, 2048 * h:2048 * h + 2048], in_=X[r0 + P * h:r0 + P * h + P, :])
+                two = (x0_jobs + x1_jobs)[2 * n:2 * n + 2]
+            else:
+                src = X[r0:r0 + 256, :].rearrange("(rb j) k -> j rb k", j=32)
+                for a in range(4):
+                    quad_load(raw, src, a)
+                two = [xjobs[2 * n - 4], xjobs[2 * n - 3]]
+            two[0]["words"] = words[:, 0:1024]
+            two[1]["words"] = words[:, 1024:2048]
 
         def pe_sort(job):
+            if job["kind"] == "P1A":
+                srt = sbt([P, 1024], F32, "ovl", 8, 256)
+                nc.vector.tensor_copy(
+                    out=srt[:].rearrange("p (g u q) -> p g u q", g=4, u=2, q=P),
+                    in_=job["words"].rearrange("p (g q u) -> p g u q", g=4, q=P, u=2),
+                )
+                job["srt"] = srt
+                load_next_h()
             if job["kind"] == "P1":
-                srt = sbt([P, 1024], F32, "ovl", 8)
+                srt = sbt([P, 1024], F32, "ovl", 8, 256)
                 for u in range(2):
                     nc.vector.tensor_copy(
                         out=srt[:].rearrange("p (g u a i) -> p u g a i", g=4, u=2, a=4, i=32)[:, u],
                         in_=job["words"].rearrange("p (a g i u) -> p u g a i", a=4, g=4, i=32, u=2)[:, u],
                     )
                 job["srt"] = srt
-                load_next_h()
+                if "rows" in job:
+                    load_next_h()
+
 
         def pe_transposes(job):
             job["banks"] = []
@@ -170,7 +189,7 @@ def tile_attention_pa_l_kernel(tc, attendee_stmts, attendee_eres, attender, W_ss
                 bank = psum.tile([P, 512], F32, name="tp", tag="m2")
                 for sl in range(4):
                     idx = 4 * hb + sl
-                    if job["kind"] == "P1":
+                    if job["kind"] != "P2":
                         src = job["srt"][:, P * idx:P * idx + P]
                     else:
                         src = job["words"][:, 256 * (idx // 2) + idx % 2:256 * (idx // 2) + 256:2]
@@ -180,7 +199,7 @@ def tile_attention_pa_l_kernel(tc, attendee_stmts, attendee_eres, attender, W_ss
                 load_next_h()
 
         def pe_copy(job):
-            grp = sbt([P, 2048], BF16, "ovl", 8)
+            grp = sbt([P, 2048], BF16, "ovl", 8, 256)
             for hb in range(2):
                 nc.scalar.copy(
                     out=grp[:].bitcast(F32)[:, 512 * hb:512 * hb + 512].rearrange("p (g r u) -> p g r u", g=2, r=P, u=2),
@@ -213,12 +232,12 @@ def tile_attention_pa_l_kernel(tc, attendee_stmts, attendee_eres, attender, W_ss
             c, G = divmod(s, 4)
             mat = chunk_src(c)[2]
             codes, sc = get_x(c)
-            wc, wsc = get_w(mat, G, t)
+            wc, wsl = get_w(mat, G, t)
             acc = psum.tile([P, 512], F32, name="m1", tag="m1")
             for g in range(4):
                 nc.tensor.matmul_mx(
-                    out=acc[:], lhsT=wc[:, P * g:P * g + P].bitcast(FP8X4), lhsT_scale=wsc[4 * g:P, :],
-                    rhs=codes[g][:].bitcast(FP8X4), rhs_scale=sc[4 * g:P, :], start=(g == 0), stop=(g == 3),
+                    out=acc[:], lhsT=wc[:, P * g:P * g + P].bitcast(FP8X4), lhsT_scale=wsl[4 * g:P, :],
+                    rhs=codes[:, 512 * g:512 * g + 512].bitcast(FP8X4), rhs_scale=sc[4 * g:P, :], start=(g == 0), stop=(g == 3),
                 )
             acc1[(s, t)] = acc
 
@@ -236,9 +255,9 @@ def tile_attention_pa_l_kernel(tc, attendee_stmts, attendee_eres, attender, W_ss
         def p_quantize(s):
             c, G = divmod(s, 4)
             if G == 0:
-                psc[c] = sbt([P, 512], U8, "psc", 2)
-            pq[(c, G)] = sbt([P, 512], U32, "pq%d" % G, 2)
-            nc.vector.quantize_mx(out=pq[(c, G)][:].bitcast(FP8X4), scales=psc[c][4 * G:P, :], in_=pGs[s][:])
+                psc[c] = sbt([P, 512], U8, "psc", 2, 256)
+                pq[c] = sbt([P, 2048], U32, "pq", 2, 256)
+            nc.vector.quantize_mx(out=pq[c][:, 512 * G:512 * G + 512].bitcast(FP8X4), scales=psc[c][4 * G:P, :], in_=pGs[s][:])
 
         def m2(s, ar):
             c, tt = divmod(s, 4)
@@ -246,8 +265,8 @@ def tile_attention_pa_l_kernel(tc, attendee_stmts, attendee_eres, attender, W_ss
             for G in range(4):
                 ac, asl = get_a(G, ar)
                 nc.tensor.matmul_mx(
-                    out=acc[:], lhsT=pq[(c, G)][:, P * tt:P * tt + P].bitcast(FP8X4), lhsT_scale=psc[c][4 * G:P, P * tt:P * tt + P],
-                    rhs=ac[:].bitcast(FP8X4), rhs_scale=asl[4 * G:P, :], start=(G == 0), stop=(G == 3),
+                    out=acc[:], lhsT=pq[c][:, 512 * G + P * tt:512 * G + P * tt + P].bitcast(FP8X4), lhsT_scale=psc[c][4 * G:P, P * tt:P * tt + P],
+                    rhs=ac.bitcast(FP8X4), rhs_scale=asl[4 * G:P, :], start=(G == 0), stop=(G == 3),
                 )
             acc2[(s, ar)] = acc
 
@@ -258,16 +277,15 @@ def tile_attention_pa_l_kernel(tc, attendee_stmts, attendee_eres, attender, W_ss
             nc.scalar.copy(out=ob[:], in_=acc2[(s, ar)][:])
             nc.sync.dma_start(out=out[r0 + P * tt:r0 + P * tt + P, 512 * ar:512 * ar + 512], in_=ob[:])
 
+        load_next_x()
+        load_next_x()
         for n in range(NRAWH):
             load_next_h()
-        load_pair(0)
 
         for sig in range(-8, 4 * NSTEP):
             s, j = divmod(sig, 4)
-            if sig == -2:
-                load_pair(1)
-            if sig == 4:
-                load_pair(2)
+            if sig in XLOADS:
+                load_next_x()
             for job in by_sig.get(sig, []):
                 pe_sort(job)
             for job in by_sig.get(sig - 2, []):
@@ -310,5 +328,5 @@ def tile_attention_pa_l_kernel(tc, attendee_stmts, attendee_eres, attender, W_ss
                 v_sort(wn, j - 2)
                 if j == 3:
                     load_next_h()
-            if j == 2 and s >= 0 and s % 2 == 0:
-                load_pair(s // 2 + 3)
+            if j == 2 and s >= 4 and s % 2 == 0:
+                load_next_x()

@@ -15,9 +15,10 @@ NCH = 12
 LAG = 5
 NSTEP = 4 * NCH + LAG
 WES0 = 12
-NRAWH = 6
+NRAWH = 8
+NOB = 8
 A_KINDS = ("P2", "P2")
-XLOADS = (1, 3, 6, 12, 16)
+XLOADS = (1, 3, 7, 9)
 FLOPS = 2 * 2 * (4096 + 2048) * 2048 * 2048
 
 
@@ -55,26 +56,26 @@ def tile_attention_pa_l_kernel(tc, attendee_stmts, attendee_eres, attender, W_ss
 
         def get_x(c):
             if c not in xq:
-                xq[c] = (sbt([P, 2048], U32, "xq", 2, 256), sbt([P, 512], U8, "xsc", 2, 256))
+                xq[c] = (sbt([P, 2048], U32, "xq", 2), sbt([P, 512], U8, "xsc", 2))
             return xq[c]
 
-        wsc = [sbt([P, 16 * 256], U8, "ws0", 1, 256), sbt([P, 16 * 256], U8, "ws1", 1, 256)]
+        wsc = [sbt([P, 16 * P], U8, "ws0", 1), sbt([P, 16 * P], U8, "ws1", 1)]
 
         def get_w(mat, G, t):
-            sc = wsc[mat][:, 256 * (4 * G + t):256 * (4 * G + t) + P]
+            sc = wsc[mat][:, P * (4 * G + t):P * (4 * G + t) + P]
             if mat == 0:
                 if (mat, G) not in wq:
-                    wq[(mat, G)] = sbt([P, 2048], U32, "wq0_%d" % G, 1, 256)
+                    wq[(mat, G)] = sbt([P, 2048], U32, "wq0_%d" % G, 1)
                 return wq[(mat, G)][:, 512 * t:512 * t + 512], sc
             if (mat, G, t // 2) not in wq:
-                wq[(mat, G, t // 2)] = sbt([P, 1024], U32, "ovl", 8, 256)
+                wq[(mat, G, t // 2)] = sbt([P, 1024], U32, "ovl", 8)
             return wq[(mat, G, t // 2)][:, 512 * (t % 2):512 * (t % 2) + 512], sc
 
-        asc = sbt([P, 2048], U8, "asc", 1, 256)
+        asc = sbt([P, 2048], U8, "asc", 1)
 
         def get_a(G, ar):
             if ar not in aq:
-                aq[ar] = sbt([P, 2048], U32, "aq%d" % ar, 1, 256)
+                aq[ar] = sbt([P, 2048], U32, "aq%d" % ar, 1)
             return aq[ar][:, 512 * G:512 * G + 512], asc[:, 512 * ar:512 * ar + 512]
 
         def dest(d, g):
@@ -119,8 +120,7 @@ def tile_attention_pa_l_kernel(tc, attendee_stmts, attendee_eres, attender, W_ss
             xjobs[v] = {"kind": "V", "dest": ("x", 1 + v // 4, v % 4), "pair": v // 2, "half": v % 2}
 
         def quad_load(raw, src, a):
-            eng = nc.sync if a < 2 else nc.scalar
-            eng.dma_start(out=raw[32 * a:32 * a + 32, :].rearrange("p (rb k) -> p rb k", k=512), in_=src[:, :, 512 * a:512 * a + 512])
+            nc.sync.dma_start(out=raw[32 * a:32 * a + 32, :].rearrange("p (rb k) -> p rb k", k=512), in_=src[:, :, 512 * a:512 * a + 512])
 
         hqueue = w_jobs + a_jobs + [wjobs[WES0 + w] for w in range(16)]
         hstate = {"next": 0}
@@ -133,7 +133,7 @@ def tile_attention_pa_l_kernel(tc, attendee_stmts, attendee_eres, attender, W_ss
             job = hqueue[n]
             raw = sbt([P, 2048], BF16, "rawh", NRAWH)
             if job["kind"] == "V":
-                for a in range(4):
+                for a in (0, 2, 1, 3):
                     quad_load(raw, job["wsrc"], a)
             else:
                 nc.sync.dma_start(out=raw[:], in_=job["rows"])
@@ -148,7 +148,7 @@ def tile_attention_pa_l_kernel(tc, attendee_stmts, attendee_eres, attender, W_ss
             xstate["next"] = n + 1
             X, r0, mat, out = chunk_src(n // 2)
             r0 = r0 + 256 * (n % 2)
-            raw = sbt([P, 4096], BF16, "rawx", 3)
+            raw = sbt([P, 4096], BF16, "rawx", 2)
             words = raw[:].bitcast(F32)
             if n < 4:
                 for h in range(2):
@@ -156,7 +156,7 @@ def tile_attention_pa_l_kernel(tc, attendee_stmts, attendee_eres, attender, W_ss
                 two = (x0_jobs + x1_jobs)[2 * n:2 * n + 2]
             else:
                 src = X[r0:r0 + 256, :].rearrange("(rb j) k -> j rb k", j=32)
-                for a in range(4):
+                for a in (0, 2, 1, 3):
                     quad_load(raw, src, a)
                 two = [xjobs[2 * n - 4], xjobs[2 * n - 3]]
             two[0]["words"] = words[:, 0:1024]
@@ -164,7 +164,7 @@ def tile_attention_pa_l_kernel(tc, attendee_stmts, attendee_eres, attender, W_ss
 
         def pe_sort(job):
             if job["kind"] == "P1A":
-                srt = sbt([P, 1024], F32, "ovl", 8, 256)
+                srt = sbt([P, 1024], F32, "ovl", 8)
                 nc.vector.tensor_copy(
                     out=srt[:].rearrange("p (g u q) -> p g u q", g=4, u=2, q=P),
                     in_=job["words"].rearrange("p (g q u) -> p g u q", g=4, q=P, u=2),
@@ -172,7 +172,7 @@ def tile_attention_pa_l_kernel(tc, attendee_stmts, attendee_eres, attender, W_ss
                 job["srt"] = srt
                 load_next_h()
             if job["kind"] == "P1":
-                srt = sbt([P, 1024], F32, "ovl", 8, 256)
+                srt = sbt([P, 1024], F32, "ovl", 8)
                 for u in range(2):
                     nc.vector.tensor_copy(
                         out=srt[:].rearrange("p (g u a i) -> p u g a i", g=4, u=2, a=4, i=32)[:, u],
@@ -199,7 +199,7 @@ def tile_attention_pa_l_kernel(tc, attendee_stmts, attendee_eres, attender, W_ss
                 load_next_h()
 
         def pe_copy(job):
-            grp = sbt([P, 2048], BF16, "ovl", 8, 256)
+            grp = sbt([P, 2048], BF16, "ovl", 8)
             for hb in range(2):
                 nc.scalar.copy(
                     out=grp[:].bitcast(F32)[:, 512 * hb:512 * hb + 512].rearrange("p (g r u) -> p g r u", g=2, r=P, u=2),
@@ -255,8 +255,8 @@ def tile_attention_pa_l_kernel(tc, attendee_stmts, attendee_eres, attender, W_ss
         def p_quantize(s):
             c, G = divmod(s, 4)
             if G == 0:
-                psc[c] = sbt([P, 512], U8, "psc", 2, 256)
-                pq[c] = sbt([P, 2048], U32, "pq", 2, 256)
+                psc[c] = sbt([P, 512], U8, "psc", 2)
+                pq[c] = sbt([P, 2048], U32, "pq", 2)
             nc.vector.quantize_mx(out=pq[c][:, 512 * G:512 * G + 512].bitcast(FP8X4), scales=psc[c][4 * G:P, :], in_=pGs[s][:])
 
         def m2(s, ar):
@@ -273,7 +273,7 @@ def tile_attention_pa_l_kernel(tc, attendee_stmts, attendee_eres, attender, W_ss
         def e2(s, ar):
             c, tt = divmod(s, 4)
             X, r0, mat, out = chunk_src(c)
-            ob = sbt([P, 512], F32, "ob", 4)
+            ob = sbt([P, 512], F32, "ob", NOB)
             nc.scalar.copy(out=ob[:], in_=acc2[(s, ar)][:])
             nc.sync.dma_start(out=out[r0 + P * tt:r0 + P * tt + P, 512 * ar:512 * ar + 512], in_=ob[:])
 

@@ -262,7 +262,7 @@ def tile_attention_pa_l_kernel(tc, attendee_stmts, attendee_eres, attender, W_ss
         def m2(s, ar):
             c, tt = divmod(s, 4)
             acc = psum.tile([P, 512], F32, name="m2", tag="m2")
-            for G in range(4):
+            for G in (list(range(4)) * (2 if 8 <= s < 40 else 1)):
                 ac, asl = get_a(G, ar)
                 nc.tensor.matmul_mx(
                     out=acc[:], lhsT=pq[c][:, 512 * G + P * tt:512 * G + P * tt + P].bitcast(FP8X4), lhsT_scale=psc[c][4 * G:P, P * tt:P * tt + P],

@@ -8,17 +8,18 @@ BF16 = mybir.dt.bfloat16
 U32 = mybir.dt.uint32
 U8 = mybir.dt.uint8
 FP8X4 = mybir.dt.float8_e4m3fn_x4
-IDENT = mybir.ActivationFunctionType.Identity
+IDENTITY = mybir.ActivationFunctionType.Identity
 
 P = 128
-NCH = 12
+CHUNKS = 12
+STEPS1 = 4 * CHUNKS
 LAG = 5
-NSTEP = 4 * NCH + LAG
-WES0 = 12
-NRAWH = 8
-NOB = 8
-A_KINDS = ("P2", "P2")
-XLOADS = (1, 3, 7, 9)
+W_ES_FIRST_STEP = 12
+ROW_BUFS = 8
+OUT_BUFS = 8
+SHARED_BUFS = 8
+EARLY_PAIR_SLOTS = (1, 3, 7, 9)
+
 FLOPS = 2 * 2 * (4096 + 2048) * 2048 * 2048
 
 
@@ -28,305 +29,292 @@ def tile_attention_pa_l_kernel(tc, attendee_stmts, attendee_eres, attender, W_ss
         sb = ctx.enter_context(tc.tile_pool(name="sb", bufs=1))
         psum = ctx.enter_context(tc.psum_pool(name="psum", bufs=4))
 
-        def sbt(shape, dtype, tag, bufs, align=64):
-            return sb.tile(shape, dtype, name=tag, tag=tag, bufs=bufs, align_bytes=align)
+        def sb_tile(shape, dtype, tag, bufs):
+            return sb.tile(shape, dtype, name=tag, tag=tag, bufs=bufs, align_bytes=64)
 
-        def chunk_src(c):
+        def chunk_info(c):
             if c < 8:
                 return attendee_stmts, 512 * c, 0, out_0
             return attendee_eres, 512 * (c - 8), 1, out_1
 
-        ident = sbt([P, P], F32, "ident", 1)
+        ident = sb_tile([P, P], F32, "ident", 1)
         make_identity(nc, ident[:])
-        warm = sbt([P, 1], F32, "warm", 1)
-        warm2 = sbt([P, 1], F32, "warm2", 1)
+        warm = sb_tile([P, 1], F32, "warm", 1)
+        warm2 = sb_tile([P, 1], F32, "warm2", 1)
         nc.vector.memset(warm[:], 0.0)
-        nc.scalar.activation(out=warm2[:], in_=warm[:], func=IDENT)
+        nc.scalar.activation(out=warm2[:], in_=warm[:], func=IDENTITY)
         bias = []
-        for mat, b in enumerate((b_ss, b_es)):
-            braw = sbt([P, 16], BF16, "braw%d" % mat, 1)
+        for m, b in enumerate((b_ss, b_es)):
+            braw = sb_tile([P, 16], BF16, "braw%d" % m, 1)
             nc.scalar.dma_start(out=braw[:].rearrange("c (G t) -> c G t", t=4), in_=b.rearrange("(G c t) -> c G t", G=4, c=P, t=4))
-            bf = sbt([P, 16], F32, "bias%d" % mat, 1)
-            nc.vector.tensor_copy(out=bf[:], in_=braw[:])
-            bias.append(bf)
+            bias_f32 = sb_tile([P, 16], F32, "bias%d" % m, 1)
+            nc.vector.tensor_copy(out=bias_f32[:], in_=braw[:])
+            bias.append(bias_f32)
 
         ctx.enter_context(tc.manual_schedule())
 
-        xq, pq, psc, wq, aq = {}, {}, {}, {}, {}
+        x_tiles, p_codes, p_scales, w_tiles, a_tiles = {}, {}, {}, {}, {}
 
-        def get_x(c):
-            if c not in xq:
-                xq[c] = (sbt([P, 2048], U32, "xq", 2), sbt([P, 512], U8, "xsc", 2))
-            return xq[c]
+        def x_operand(c):
+            if c not in x_tiles:
+                x_tiles[c] = (sb_tile([P, 2048], U32, "xq", 2), sb_tile([P, 512], U8, "xsc", 2))
+            return x_tiles[c]
 
-        wsc = [sbt([P, 16 * P], U8, "ws0", 1), sbt([P, 16 * P], U8, "ws1", 1)]
+        w_scales = [sb_tile([P, 16 * P], U8, "ws0", 1), sb_tile([P, 16 * P], U8, "ws1", 1)]
 
-        def get_w(mat, G, t):
-            sc = wsc[mat][:, P * (4 * G + t):P * (4 * G + t) + P]
-            if mat == 0:
-                if (mat, G) not in wq:
-                    wq[(mat, G)] = sbt([P, 2048], U32, "wq0_%d" % G, 1)
-                return wq[(mat, G)][:, 512 * t:512 * t + 512], sc
-            if (mat, G, t // 2) not in wq:
-                wq[(mat, G, t // 2)] = sbt([P, 1024], U32, "ovl", 8)
-            return wq[(mat, G, t // 2)][:, 512 * (t % 2):512 * (t % 2) + 512], sc
+        def w_operand(m, G, t):
+            scales = w_scales[m][:, P * (4 * G + t):P * (4 * G + t) + P]
+            if m == 0:
+                if (m, G) not in w_tiles:
+                    w_tiles[(m, G)] = sb_tile([P, 2048], U32, "wq0_%d" % G, 1)
+                return w_tiles[(m, G)][:, 512 * t:512 * t + 512], scales
+            if (m, G, t // 2) not in w_tiles:
+                w_tiles[(m, G, t // 2)] = sb_tile([P, 1024], U32, "ovl", SHARED_BUFS)
+            return w_tiles[(m, G, t // 2)][:, 512 * (t % 2):512 * (t % 2) + 512], scales
 
-        asc = sbt([P, 2048], U8, "asc", 1)
+        a_scales = sb_tile([P, 2048], U8, "asc", 1)
 
-        def get_a(G, ar):
-            if ar not in aq:
-                aq[ar] = sbt([P, 2048], U32, "aq%d" % ar, 1)
-            return aq[ar][:, 512 * G:512 * G + 512], asc[:, 512 * ar:512 * ar + 512]
+        def a_operand(G, n):
+            if n not in a_tiles:
+                a_tiles[n] = sb_tile([P, 2048], U32, "aq%d" % n, 1)
+            return a_tiles[n][:, 512 * G:512 * G + 512], a_scales[:, 512 * n:512 * n + 512]
 
-        def dest(d, g):
-            if d[0] == "x":
-                codes, sc = get_x(d[1])
-                lo = P * d[2]
-                return codes[:, 512 * g + lo:512 * g + lo + P], sc[4 * g:P, lo:lo + P]
-            if d[0] == "w":
-                codes, sc = get_w(d[1], d[2], d[3])
-                return codes[:, P * g:P * g + P], sc[4 * g:P, :]
-            codes, sc = get_a(g, d[1] // 4)
-            lo = P * (d[1] % 4)
-            return codes[:, lo:lo + P], sc[4 * g:P, lo:lo + P]
+        def job_target(target, g):
+            if target[0] == "x":
+                codes, scales = x_operand(target[1])
+                lo = P * target[2]
+                return codes[:, 512 * g + lo:512 * g + lo + P], scales[4 * g:P, lo:lo + P]
+            if target[0] == "w":
+                codes, scales = w_operand(target[1], target[2], target[3])
+                return codes[:, P * g:P * g + P], scales[4 * g:P, :]
+            codes, scales = a_operand(g, target[1] // 4)
+            lo = P * (target[1] % 4)
+            return codes[:, lo:lo + P], scales[4 * g:P, lo:lo + P]
 
         def quantize(job):
             for g in range(4):
-                codes, sc = dest(job["dest"], g)
-                nc.vector.quantize_mx(out=codes.bitcast(FP8X4), scales=sc, in_=job["grp"][:, 512 * g:512 * g + 512])
+                codes, scales = job_target(job["target"], g)
+                nc.vector.quantize_mx(out=codes.bitcast(FP8X4), scales=scales, in_=job["grouped"][:, 512 * g:512 * g + 512])
 
-        x0_jobs, x1_jobs, w_jobs, a_jobs = [], [], [], []
-        for rt in range(4):
-            x0_jobs.append({"kind": "P1", "dest": ("x", 0, rt), "last": rt % 2 == 1})
-            x1_jobs.append({"kind": "P1", "dest": ("x", 1, rt), "last": rt % 2 == 1})
-        wss_view = W_ss.rearrange("(G c t) k -> G t c k", G=4, c=P, t=4)
+        x0_jobs, x1_jobs, w_ss_jobs, a_jobs = [], [], [], []
+        for r in range(4):
+            x0_jobs.append({"target": ("x", 0, r), "order": 1})
+            x1_jobs.append({"target": ("x", 1, r), "order": 1})
+        w_ss_rows = W_ss.rearrange("(G c t) k -> G t c k", G=4, c=P, t=4)
         for G in range(4):
             for t in range(4):
-                w_jobs.append({"kind": "P1", "rows": wss_view[G, t], "dest": ("w", 0, G, t)})
-        for at in range(16):
-            a_jobs.append({"kind": A_KINDS[at % 2], "rows": attender[P * at:P * at + P, :], "dest": ("a", at)})
-        pe_jobs = x0_jobs + w_jobs + x1_jobs + a_jobs
-        by_sig = {}
-        for n, job in enumerate(pe_jobs):
-            sg = n - 8 if n < 8 else (n - 8) // 2
-            by_sig[sg] = by_sig.get(sg, []) + [job]
+                w_ss_jobs.append({"target": ("w", 0, G, t), "order": 1, "rows": w_ss_rows[G, t]})
+        for r in range(16):
+            a_jobs.append({"target": ("a", r), "order": 2, "rows": attender[P * r:P * r + P, :]})
+        tensor_jobs = {}
+        for n, job in enumerate(x0_jobs + w_ss_jobs + x1_jobs + a_jobs):
+            slot = n - 8 if n < 8 else (n - 8) // 2
+            tensor_jobs[slot] = tensor_jobs.get(slot, []) + [job]
 
-        wes_view = W_es.rearrange("(G rb j t) k -> G t j rb k", G=4, rb=4, j=32, t=4)
-        wjobs = {}
-        for w in range(16):
-            wjobs[WES0 + w] = {"kind": "V", "dest": ("w", 1, w // 4, w % 4), "wsrc": wes_view[w // 4, w % 4]}
-        xjobs = {}
-        for v in range(4, 44):
-            xjobs[v] = {"kind": "V", "dest": ("x", 1 + v // 4, v % 4), "pair": v // 2, "half": v % 2}
+        w_es_rows = W_es.rearrange("(G rb j t) k -> G t j rb k", G=4, rb=4, j=32, t=4)
+        w_es_jobs = {}
+        for n in range(16):
+            w_es_jobs[W_ES_FIRST_STEP + n] = {"target": ("w", 1, n // 4, n % 4), "quadrant_rows": w_es_rows[n // 4, n % 4]}
+        x_jobs = {}
+        for step in range(4, 44):
+            x_jobs[step] = {"target": ("x", 1 + step // 4, step % 4)}
 
-        def quad_load(raw, src, a):
-            nc.sync.dma_start(out=raw[32 * a:32 * a + 32, :].rearrange("p (rb k) -> p rb k", k=512), in_=src[:, :, 512 * a:512 * a + 512])
+        def load_quadrants(raw, rows):
+            for a in (0, 2, 1, 3):
+                nc.sync.dma_start(out=raw[32 * a:32 * a + 32, :].rearrange("p (rb k) -> p rb k", k=512), in_=rows[:, :, 512 * a:512 * a + 512])
 
-        hqueue = w_jobs + a_jobs + [wjobs[WES0 + w] for w in range(16)]
-        hstate = {"next": 0}
+        row_queue = w_ss_jobs + a_jobs + [w_es_jobs[W_ES_FIRST_STEP + n] for n in range(16)]
+        loaded = {"rows": 0, "pairs": 0}
 
-        def load_next_h():
-            n = hstate["next"]
-            if n >= len(hqueue):
+        def load_next_rows():
+            n = loaded["rows"]
+            if n >= len(row_queue):
                 return
-            hstate["next"] = n + 1
-            job = hqueue[n]
-            raw = sbt([P, 2048], BF16, "rawh", NRAWH)
-            if job["kind"] == "V":
-                for a in (0, 2, 1, 3):
-                    quad_load(raw, job["wsrc"], a)
-            else:
+            loaded["rows"] = n + 1
+            job = row_queue[n]
+            raw = sb_tile([P, 2048], BF16, "rawh", ROW_BUFS)
+            if "rows" in job:
                 nc.sync.dma_start(out=raw[:], in_=job["rows"])
+            else:
+                load_quadrants(raw, job["quadrant_rows"])
             job["words"] = raw[:].bitcast(F32)
 
-        xstate = {"next": 0}
-
-        def load_next_x():
-            n = xstate["next"]
-            if n >= 24:
+        def load_next_pair():
+            n = loaded["pairs"]
+            if n >= 2 * CHUNKS:
                 return
-            xstate["next"] = n + 1
-            X, r0, mat, out = chunk_src(n // 2)
+            loaded["pairs"] = n + 1
+            rows, r0, m, out = chunk_info(n // 2)
             r0 = r0 + 256 * (n % 2)
-            raw = sbt([P, 4096], BF16, "rawx", 2)
+            raw = sb_tile([P, 4096], BF16, "rawx", 2)
             words = raw[:].bitcast(F32)
             if n < 4:
                 for h in range(2):
-                    nc.sync.dma_start(out=raw[:, 2048 * h:2048 * h + 2048], in_=X[r0 + P * h:r0 + P * h + P, :])
+                    nc.sync.dma_start(out=raw[:, 2048 * h:2048 * h + 2048], in_=rows[r0 + P * h:r0 + P * h + P, :])
                 two = (x0_jobs + x1_jobs)[2 * n:2 * n + 2]
             else:
-                src = X[r0:r0 + 256, :].rearrange("(rb j) k -> j rb k", j=32)
-                for a in (0, 2, 1, 3):
-                    quad_load(raw, src, a)
-                two = [xjobs[2 * n - 4], xjobs[2 * n - 3]]
+                load_quadrants(raw, rows[r0:r0 + 256, :].rearrange("(rb j) k -> j rb k", j=32))
+                two = [x_jobs[2 * n - 4], x_jobs[2 * n - 3]]
             two[0]["words"] = words[:, 0:1024]
             two[1]["words"] = words[:, 1024:2048]
 
-        def pe_sort(job):
-            if job["kind"] == "P1A":
-                srt = sbt([P, 1024], F32, "ovl", 8)
-                nc.vector.tensor_copy(
-                    out=srt[:].rearrange("p (g u q) -> p g u q", g=4, u=2, q=P),
-                    in_=job["words"].rearrange("p (g q u) -> p g u q", g=4, q=P, u=2),
-                )
-                job["srt"] = srt
-                load_next_h()
-            if job["kind"] == "P1":
-                srt = sbt([P, 1024], F32, "ovl", 8)
+        def tensor_sort(job):
+            srt = sb_tile([P, 1024], F32, "ovl", SHARED_BUFS)
+            if job["order"] == 1:
                 for u in range(2):
                     nc.vector.tensor_copy(
                         out=srt[:].rearrange("p (g u a i) -> p u g a i", g=4, u=2, a=4, i=32)[:, u],
                         in_=job["words"].rearrange("p (a g i u) -> p u g a i", a=4, g=4, i=32, u=2)[:, u],
                     )
-                job["srt"] = srt
-                if "rows" in job:
-                    load_next_h()
-
-
-        def pe_transposes(job):
-            job["banks"] = []
-            for hb in range(2):
-                bank = psum.tile([P, 512], F32, name="tp", tag="m2")
-                for sl in range(4):
-                    idx = 4 * hb + sl
-                    if job["kind"] != "P2":
-                        src = job["srt"][:, P * idx:P * idx + P]
-                    else:
-                        src = job["words"][:, 256 * (idx // 2) + idx % 2:256 * (idx // 2) + 256:2]
-                    nc.tensor.transpose(out=bank[:, P * sl:P * sl + P], in_=src, identity=ident[:])
-                job["banks"].append(bank)
-            if job["kind"] == "P2":
-                load_next_h()
-
-        def pe_copy(job):
-            grp = sbt([P, 2048], BF16, "ovl", 8)
-            for hb in range(2):
-                nc.scalar.copy(
-                    out=grp[:].bitcast(F32)[:, 512 * hb:512 * hb + 512].rearrange("p (g r u) -> p g r u", g=2, r=P, u=2),
-                    in_=job["banks"][hb][:].rearrange("p (g u r) -> p g r u", g=2, u=2, r=P),
+            else:
+                nc.vector.tensor_copy(
+                    out=srt[:].rearrange("p (g u q) -> p g u q", g=4, u=2, q=P),
+                    in_=job["words"].rearrange("p (g q u) -> p g u q", g=4, q=P, u=2),
                 )
-            job["grp"] = grp
+            job["sorted"] = srt
+            if "rows" in job:
+                load_next_rows()
 
-        def v_sort(job, u):
+        def tensor_transpose(job):
+            job["banks"] = []
+            for h in range(2):
+                bank = psum.tile([P, 512], F32, name="tp", tag="m2")
+                for n in range(4):
+                    lo = P * (4 * h + n)
+                    nc.tensor.transpose(out=bank[:, P * n:P * n + P], in_=job["sorted"][:, lo:lo + P], identity=ident[:])
+                job["banks"].append(bank)
+
+        def tensor_copy_out(job):
+            grouped = sb_tile([P, 2048], BF16, "ovl", SHARED_BUFS)
+            for h in range(2):
+                nc.scalar.copy(
+                    out=grouped[:].bitcast(F32)[:, 512 * h:512 * h + 512].rearrange("p (g r u) -> p g r u", g=2, r=P, u=2),
+                    in_=job["banks"][h][:].rearrange("p (g u r) -> p g r u", g=2, u=2, r=P),
+                )
+            job["grouped"] = grouped
+
+        def vector_sort(job, u):
             if u == 0:
-                job["srt"] = sbt([P, 1024], F32, "srtv", 3)
+                job["sorted"] = sb_tile([P, 1024], F32, "srtv", 3)
             nc.scalar.copy(
-                out=job["srt"][:].rearrange("p (g rb u i) -> p u g rb i", g=4, rb=4, u=2, i=32)[:, u],
+                out=job["sorted"][:].rearrange("p (g rb u i) -> p u g rb i", g=4, rb=4, u=2, i=32)[:, u],
                 in_=job["words"].rearrange("p (rb g i u) -> p u g rb i", rb=4, g=4, i=32, u=2)[:, u],
             )
 
-        def v_tr(job):
-            job["trn"] = sbt([P, 1024], F32, "trn", 1)
-            nc.vector.transpose(out=job["trn"][:], in_=job["srt"][:])
+        def vector_transpose(job):
+            job["turned"] = sb_tile([P, 1024], F32, "trn", 1)
+            nc.vector.transpose(out=job["turned"][:], in_=job["sorted"][:])
 
-        def v_il(job):
-            job["grp"] = sbt([P, 2048], BF16, "grp", 2)
+        def vector_interleave(job):
+            job["grouped"] = sb_tile([P, 2048], BF16, "grp", 2)
             nc.vector.tensor_copy(
-                out=job["grp"][:].bitcast(F32).rearrange("p (x j u) -> p x j u", x=16, j=32, u=2),
-                in_=job["trn"][:].rearrange("p (x u j) -> p x j u", x=16, u=2, j=32),
+                out=job["grouped"][:].bitcast(F32).rearrange("p (x j u) -> p x j u", x=16, j=32, u=2),
+                in_=job["turned"][:].rearrange("p (x u j) -> p x j u", x=16, u=2, j=32),
             )
 
-        acc1, acc2, pTs, pGs = {}, {}, {}, {}
+        acc1, acc2, p_rounded, p_grouped = {}, {}, {}, {}
 
-        def m1(s, t):
+        def stage1_matmuls(s, t):
             c, G = divmod(s, 4)
-            mat = chunk_src(c)[2]
-            codes, sc = get_x(c)
-            wc, wsl = get_w(mat, G, t)
+            x_codes, x_scales = x_operand(c)
+            w_codes, w_sc = w_operand(chunk_info(c)[2], G, t)
             acc = psum.tile([P, 512], F32, name="m1", tag="m1")
             for g in range(4):
                 nc.tensor.matmul_mx(
-                    out=acc[:], lhsT=wc[:, P * g:P * g + P].bitcast(FP8X4), lhsT_scale=wsl[4 * g:P, :],
-                    rhs=codes[:, 512 * g:512 * g + 512].bitcast(FP8X4), rhs_scale=sc[4 * g:P, :], start=(g == 0), stop=(g == 3),
+                    out=acc[:], lhsT=w_codes[:, P * g:P * g + P].bitcast(FP8X4), lhsT_scale=w_sc[4 * g:P, :],
+                    rhs=x_codes[:, 512 * g:512 * g + 512].bitcast(FP8X4), rhs_scale=x_scales[4 * g:P, :], start=(g == 0), stop=(g == 3),
                 )
             acc1[(s, t)] = acc
 
-        def e1(s, t):
+        def stage1_bias_round(s, t):
             c, G = divmod(s, 4)
-            mat = chunk_src(c)[2]
             if t == 0:
-                pTs[s] = sbt([P, 4, 512], BF16, "pT", 2)
-            nc.scalar.activation(out=pTs[s][:, t, :], in_=acc1[(s, t)][:], func=IDENT, bias=bias[mat][:, 4 * G + t:4 * G + t + 1])
+                p_rounded[s] = sb_tile([P, 4, 512], BF16, "pT", 2)
+            nc.scalar.activation(out=p_rounded[s][:, t, :], in_=acc1[(s, t)][:], func=IDENTITY, bias=bias[chunk_info(c)[2]][:, 4 * G + t:4 * G + t + 1])
 
         def p_interleave(s):
-            pGs[s] = sbt([P, 2048], BF16, "pG", 1)
-            nc.vector.tensor_copy(out=pGs[s][:].rearrange("p (n t) -> p n t", t=4), in_=pTs[s][:].rearrange("p t n -> p n t"))
+            p_grouped[s] = sb_tile([P, 2048], BF16, "pG", 1)
+            nc.vector.tensor_copy(out=p_grouped[s][:].rearrange("p (n t) -> p n t", t=4), in_=p_rounded[s][:].rearrange("p t n -> p n t"))
 
         def p_quantize(s):
             c, G = divmod(s, 4)
             if G == 0:
-                psc[c] = sbt([P, 512], U8, "psc", 2)
-                pq[c] = sbt([P, 2048], U32, "pq", 2)
-            nc.vector.quantize_mx(out=pq[c][:, 512 * G:512 * G + 512].bitcast(FP8X4), scales=psc[c][4 * G:P, :], in_=pGs[s][:])
+                p_scales[c] = sb_tile([P, 512], U8, "psc", 2)
+                p_codes[c] = sb_tile([P, 2048], U32, "pq", 2)
+            nc.vector.quantize_mx(out=p_codes[c][:, 512 * G:512 * G + 512].bitcast(FP8X4), scales=p_scales[c][4 * G:P, :], in_=p_grouped[s][:])
 
-        def m2(s, ar):
-            c, tt = divmod(s, 4)
+        def stage2_matmuls(s, n):
+            c, r = divmod(s, 4)
             acc = psum.tile([P, 512], F32, name="m2", tag="m2")
-            for G in (list(range(4)) * (2 if 8 <= s < 40 else 1)):
-                ac, asl = get_a(G, ar)
+            for G in range(4):
+                a_codes, a_sc = a_operand(G, n)
+                lo = 512 * G + P * r
                 nc.tensor.matmul_mx(
-                    out=acc[:], lhsT=pq[c][:, 512 * G + P * tt:512 * G + P * tt + P].bitcast(FP8X4), lhsT_scale=psc[c][4 * G:P, P * tt:P * tt + P],
-                    rhs=ac.bitcast(FP8X4), rhs_scale=asl[4 * G:P, :], start=(G == 0), stop=(G == 3),
+                    out=acc[:], lhsT=p_codes[c][:, lo:lo + P].bitcast(FP8X4), lhsT_scale=p_scales[c][4 * G:P, P * r:P * r + P],
+                    rhs=a_codes.bitcast(FP8X4), rhs_scale=a_sc[4 * G:P, :], start=(G == 0), stop=(G == 3),
                 )
-            acc2[(s, ar)] = acc
+            acc2[(s, n)] = acc
 
-        def e2(s, ar):
-            c, tt = divmod(s, 4)
-            X, r0, mat, out = chunk_src(c)
-            ob = sbt([P, 512], F32, "ob", NOB)
-            nc.scalar.copy(out=ob[:], in_=acc2[(s, ar)][:])
-            nc.sync.dma_start(out=out[r0 + P * tt:r0 + P * tt + P, 512 * ar:512 * ar + 512], in_=ob[:])
+        def stage2_store(s, n):
+            c, r = divmod(s, 4)
+            rows, r0, m, out = chunk_info(c)
+            staged = sb_tile([P, 512], F32, "ob", OUT_BUFS)
+            nc.scalar.copy(out=staged[:], in_=acc2[(s, n)][:])
+            nc.sync.dma_start(out=out[r0 + P * r:r0 + P * r + P, 512 * n:512 * n + 512], in_=staged[:])
 
-        load_next_x()
-        load_next_x()
-        for n in range(NRAWH):
-            load_next_h()
+        load_next_pair()
+        load_next_pair()
+        for n in range(ROW_BUFS):
+            load_next_rows()
 
-        for sig in range(-8, 4 * NSTEP):
-            s, j = divmod(sig, 4)
-            if sig in XLOADS:
-                load_next_x()
-            for job in by_sig.get(sig, []):
-                pe_sort(job)
-            for job in by_sig.get(sig - 2, []):
+        for slot in range(-8, 4 * (STEPS1 + LAG)):
+            s, j = divmod(slot, 4)
+            if slot in EARLY_PAIR_SLOTS:
+                load_next_pair()
+            for job in tensor_jobs.get(slot, []):
+                tensor_sort(job)
+            for job in tensor_jobs.get(slot - 2, []):
                 quantize(job)
-            for job in by_sig.get(sig - 1, []):
-                pe_transposes(job)
-            for job in by_sig.get(sig - 1, []):
-                pe_copy(job)
-            if 0 <= s < 48:
-                m1(s, j)
-            if 0 <= s - LAG < 48:
-                m2(s - LAG, j)
-            if 0 <= s < 48:
-                e1(s, j)
-            if 0 <= s - LAG < 48:
-                e2(s - LAG, j)
-            xj, wj = xjobs.get(s), wjobs.get(s)
+            for job in tensor_jobs.get(slot - 1, []):
+                tensor_transpose(job)
+            for job in tensor_jobs.get(slot - 1, []):
+                tensor_copy_out(job)
+
+            if 0 <= s < STEPS1:
+                stage1_matmuls(s, j)
+            if 0 <= s - LAG < STEPS1:
+                stage2_matmuls(s - LAG, j)
+            if 0 <= s < STEPS1:
+                stage1_bias_round(s, j)
+            if 0 <= s - LAG < STEPS1:
+                stage2_store(s - LAG, j)
+
+            x_job, w_job = x_jobs.get(s), w_es_jobs.get(s)
             if j == 0:
-                if xj:
-                    v_tr(xj)
-                if 0 <= s - 1 < 48:
+                if x_job:
+                    vector_transpose(x_job)
+                if 0 <= s - 1 < STEPS1:
                     p_interleave(s - 1)
             if j == 1:
-                if xj:
-                    v_il(xj)
-                if 0 <= s - 1 < 48:
+                if x_job:
+                    vector_interleave(x_job)
+                if 0 <= s - 1 < STEPS1:
                     p_quantize(s - 1)
             if j == 2:
-                if wj:
-                    v_tr(wj)
-                if xj:
-                    quantize(xj)
-            if j == 3 and wj:
-                v_il(wj)
-                quantize(wj)
-            xn, wn = xjobs.get(s + 1), wjobs.get(s + 1)
-            if j < 2 and xn:
-                v_sort(xn, j)
-            if j >= 2 and wn:
-                v_sort(wn, j - 2)
+                if w_job:
+                    vector_transpose(w_job)
+                if x_job:
+                    quantize(x_job)
+            if j == 3 and w_job:
+                vector_interleave(w_job)
+                quantize(w_job)
+
+            next_x, next_w = x_jobs.get(s + 1), w_es_jobs.get(s + 1)
+            if j < 2 and next_x:
+                vector_sort(next_x, j)
+            if j >= 2 and next_w:
+                vector_sort(next_w, j - 2)
                 if j == 3:
-                    load_next_h()
+                    load_next_rows()
             if j == 2 and s >= 4 and s % 2 == 0:
-                load_next_x()
+                load_next_pair()

from contextlib import ExitStack

import concourse.mybir as mybir
from concourse.masks import make_identity

F32 = mybir.dt.float32
BF16 = mybir.dt.bfloat16
U32 = mybir.dt.uint32
U8 = mybir.dt.uint8
FP8X4 = mybir.dt.float8_e4m3fn_x4
IDENTITY = mybir.ActivationFunctionType.Identity

P = 128
CHUNKS = 12
STEPS1 = 4 * CHUNKS
LAG = 5
W_ES_FIRST_STEP = 12
ROW_BUFS = 8
OUT_BUFS = 8
SHARED_BUFS = 8
EARLY_PAIR_SLOTS = (1, 3, 7, 9)

FLOPS = 2 * 2 * (4096 + 2048) * 2048 * 2048


def tile_attention_pa_l_kernel(tc, attendee_stmts, attendee_eres, attender, W_ss, b_ss, W_es, b_es, out_0, out_1):
    nc = tc.nc
    with ExitStack() as ctx:
        sb = ctx.enter_context(tc.tile_pool(name="sb", bufs=1))
        psum = ctx.enter_context(tc.psum_pool(name="psum", bufs=4))

        def sb_tile(shape, dtype, tag, bufs):
            return sb.tile(shape, dtype, name=tag, tag=tag, bufs=bufs, align_bytes=64)

        def chunk_info(c):
            if c < 8:
                return attendee_stmts, 512 * c, 0, out_0
            return attendee_eres, 512 * (c - 8), 1, out_1

        ident = sb_tile([P, P], F32, "ident", 1)
        make_identity(nc, ident[:])
        warm = sb_tile([P, 1], F32, "warm", 1)
        warm2 = sb_tile([P, 1], F32, "warm2", 1)
        nc.vector.memset(warm[:], 0.0)
        nc.scalar.activation(out=warm2[:], in_=warm[:], func=IDENTITY)
        bias = []
        for m, b in enumerate((b_ss, b_es)):
            braw = sb_tile([P, 16], BF16, "braw%d" % m, 1)
            nc.scalar.dma_start(out=braw[:].rearrange("c (G t) -> c G t", t=4), in_=b.rearrange("(G c t) -> c G t", G=4, c=P, t=4))
            bias_f32 = sb_tile([P, 16], F32, "bias%d" % m, 1)
            nc.vector.tensor_copy(out=bias_f32[:], in_=braw[:])
            bias.append(bias_f32)

        ctx.enter_context(tc.manual_schedule())

        x_tiles, p_codes, p_scales, w_tiles, a_tiles = {}, {}, {}, {}, {}

        def x_operand(c):
            if c not in x_tiles:
                x_tiles[c] = (sb_tile([P, 2048], U32, "xq", 2), sb_tile([P, 512], U8, "xsc", 2))
            return x_tiles[c]

        w_scales = [sb_tile([P, 16 * P], U8, "ws0", 1), sb_tile([P, 16 * P], U8, "ws1", 1)]

        def w_operand(m, G, t):
            scales = w_scales[m][:, P * (4 * G + t):P * (4 * G + t) + P]
            if m == 0:
                if (m, G) not in w_tiles:
                    w_tiles[(m, G)] = sb_tile([P, 2048], U32, "wq0_%d" % G, 1)
                return w_tiles[(m, G)][:, 512 * t:512 * t + 512], scales
            if (m, G, t // 2) not in w_tiles:
                w_tiles[(m, G, t // 2)] = sb_tile([P, 1024], U32, "ovl", SHARED_BUFS)
            return w_tiles[(m, G, t // 2)][:, 512 * (t % 2):512 * (t % 2) + 512], scales

        a_scales = sb_tile([P, 2048], U8, "asc", 1)

        def a_operand(G, n):
            if n not in a_tiles:
                a_tiles[n] = sb_tile([P, 2048], U32, "aq%d" % n, 1)
            return a_tiles[n][:, 512 * G:512 * G + 512], a_scales[:, 512 * n:512 * n + 512]

        def job_target(target, g):
            if target[0] == "x":
                codes, scales = x_operand(target[1])
                lo = P * target[2]
                return codes[:, 512 * g + lo:512 * g + lo + P], scales[4 * g:P, lo:lo + P]
            if target[0] == "w":
                codes, scales = w_operand(target[1], target[2], target[3])
                return codes[:, P * g:P * g + P], scales[4 * g:P, :]
            codes, scales = a_operand(g, target[1] // 4)
            lo = P * (target[1] % 4)
            return codes[:, lo:lo + P], scales[4 * g:P, lo:lo + P]

        def quantize(job):
            for g in range(4):
                codes, scales = job_target(job["target"], g)
                nc.vector.quantize_mx(out=codes.bitcast(FP8X4), scales=scales, in_=job["grouped"][:, 512 * g:512 * g + 512])

        x0_jobs, x1_jobs, w_ss_jobs, a_jobs = [], [], [], []
        for r in range(4):
            x0_jobs.append({"target": ("x", 0, r), "order": 1})
            x1_jobs.append({"target": ("x", 1, r), "order": 1})
        w_ss_rows = W_ss.rearrange("(G c t) k -> G t c k", G=4, c=P, t=4)
        for G in range(4):
            for t in range(4):
                w_ss_jobs.append({"target": ("w", 0, G, t), "order": 1, "rows": w_ss_rows[G, t]})
        for r in range(16):
            a_jobs.append({"target": ("a", r), "order": 2, "rows": attender[P * r:P * r + P, :]})
        tensor_jobs = {}
        for n, job in enumerate(x0_jobs + w_ss_jobs + x1_jobs + a_jobs):
            slot = n - 8 if n < 8 else (n - 8) // 2
            tensor_jobs[slot] = tensor_jobs.get(slot, []) + [job]

        w_es_rows = W_es.rearrange("(G rb j t) k -> G t j rb k", G=4, rb=4, j=32, t=4)
        w_es_jobs = {}
        for n in range(16):
            w_es_jobs[W_ES_FIRST_STEP + n] = {"target": ("w", 1, n // 4, n % 4), "quadrant_rows": w_es_rows[n // 4, n % 4]}
        x_jobs = {}
        for step in range(4, 44):
            x_jobs[step] = {"target": ("x", 1 + step // 4, step % 4)}

        def load_quadrants(raw, rows):
            for a in (0, 2, 1, 3):
                nc.sync.dma_start(out=raw[32 * a:32 * a + 32, :].rearrange("p (rb k) -> p rb k", k=512), in_=rows[:, :, 512 * a:512 * a + 512])

        row_queue = w_ss_jobs + a_jobs + [w_es_jobs[W_ES_FIRST_STEP + n] for n in range(16)]
        loaded = {"rows": 0, "pairs": 0}

        def load_next_rows():
            n = loaded["rows"]
            if n >= len(row_queue):
                return
            loaded["rows"] = n + 1
            job = row_queue[n]
            raw = sb_tile([P, 2048], BF16, "rawh", ROW_BUFS)
            if "rows" in job:
                nc.sync.dma_start(out=raw[:], in_=job["rows"])
            else:
                load_quadrants(raw, job["quadrant_rows"])
            job["words"] = raw[:].bitcast(F32)

        def load_next_pair():
            n = loaded["pairs"]
            if n >= 2 * CHUNKS:
                return
            loaded["pairs"] = n + 1
            rows, r0, m, out = chunk_info(n // 2)
            r0 = r0 + 256 * (n % 2)
            raw = sb_tile([P, 4096], BF16, "rawx", 2)
            words = raw[:].bitcast(F32)
            if n < 4:
                for h in range(2):
                    nc.sync.dma_start(out=raw[:, 2048 * h:2048 * h + 2048], in_=rows[r0 + P * h:r0 + P * h + P, :])
                two = (x0_jobs + x1_jobs)[2 * n:2 * n + 2]
            else:
                load_quadrants(raw, rows[r0:r0 + 256, :].rearrange("(rb j) k -> j rb k", j=32))
                two = [x_jobs[2 * n - 4], x_jobs[2 * n - 3]]
            two[0]["words"] = words[:, 0:1024]
            two[1]["words"] = words[:, 1024:2048]

        def tensor_sort(job):
            srt = sb_tile([P, 1024], F32, "ovl", SHARED_BUFS)
            if job["order"] == 1:
                for u in range(2):
                    nc.vector.tensor_copy(
                        out=srt[:].rearrange("p (g u a i) -> p u g a i", g=4, u=2, a=4, i=32)[:, u],
                        in_=job["words"].rearrange("p (a g i u) -> p u g a i", a=4, g=4, i=32, u=2)[:, u],
                    )
            else:
                nc.vector.tensor_copy(
                    out=srt[:].rearrange("p (g u q) -> p g u q", g=4, u=2, q=P),
                    in_=job["words"].rearrange("p (g q u) -> p g u q", g=4, q=P, u=2),
                )
            job["sorted"] = srt
            if "rows" in job:
                load_next_rows()

        def tensor_transpose(job):
            job["banks"] = []
            for h in range(2):
                bank = psum.tile([P, 512], F32, name="tp", tag="m2")
                for n in range(4):
                    lo = P * (4 * h + n)
                    nc.tensor.transpose(out=bank[:, P * n:P * n + P], in_=job["sorted"][:, lo:lo + P], identity=ident[:])
                job["banks"].append(bank)

        def tensor_copy_out(job):
            grouped = sb_tile([P, 2048], BF16, "ovl", SHARED_BUFS)
            for h in range(2):
                nc.scalar.copy(
                    out=grouped[:].bitcast(F32)[:, 512 * h:512 * h + 512].rearrange("p (g r u) -> p g r u", g=2, r=P, u=2),
                    in_=job["banks"][h][:].rearrange("p (g u r) -> p g r u", g=2, u=2, r=P),
                )
            job["grouped"] = grouped

        def vector_sort(job, u):
            if u == 0:
                job["sorted"] = sb_tile([P, 1024], F32, "srtv", 3)
            nc.scalar.copy(
                out=job["sorted"][:].rearrange("p (g rb u i) -> p u g rb i", g=4, rb=4, u=2, i=32)[:, u],
                in_=job["words"].rearrange("p (rb g i u) -> p u g rb i", rb=4, g=4, i=32, u=2)[:, u],
            )

        def vector_transpose(job):
            job["turned"] = sb_tile([P, 1024], F32, "trn", 1)
            nc.vector.transpose(out=job["turned"][:], in_=job["sorted"][:])

        def vector_interleave(job):
            job["grouped"] = sb_tile([P, 2048], BF16, "grp", 2)
            nc.vector.tensor_copy(
                out=job["grouped"][:].bitcast(F32).rearrange("p (x j u) -> p x j u", x=16, j=32, u=2),
                in_=job["turned"][:].rearrange("p (x u j) -> p x j u", x=16, u=2, j=32),
            )

        acc1, acc2, p_rounded, p_grouped = {}, {}, {}, {}

        def stage1_matmuls(s, t):
            c, G = divmod(s, 4)
            x_codes, x_scales = x_operand(c)
            w_codes, w_sc = w_operand(chunk_info(c)[2], G, t)
            acc = psum.tile([P, 512], F32, name="m1", tag="m1")
            for g in range(4):
                nc.tensor.matmul_mx(
                    out=acc[:], lhsT=w_codes[:, P * g:P * g + P].bitcast(FP8X4), lhsT_scale=w_sc[4 * g:P, :],
                    rhs=x_codes[:, 512 * g:512 * g + 512].bitcast(FP8X4), rhs_scale=x_scales[4 * g:P, :], start=(g == 0), stop=(g == 3),
                )
            acc1[(s, t)] = acc

        def stage1_bias_round(s, t):
            c, G = divmod(s, 4)
            if t == 0:
                p_rounded[s] = sb_tile([P, 4, 512], BF16, "pT", 2)
            nc.scalar.activation(out=p_rounded[s][:, t, :], in_=acc1[(s, t)][:], func=IDENTITY, bias=bias[chunk_info(c)[2]][:, 4 * G + t:4 * G + t + 1])

        def p_interleave(s):
            p_grouped[s] = sb_tile([P, 2048], BF16, "pG", 1)
            nc.vector.tensor_copy(out=p_grouped[s][:].rearrange("p (n t) -> p n t", t=4), in_=p_rounded[s][:].rearrange("p t n -> p n t"))

        def p_quantize(s):
            c, G = divmod(s, 4)
            if G == 0:
                p_scales[c] = sb_tile([P, 512], U8, "psc", 2)
                p_codes[c] = sb_tile([P, 2048], U32, "pq", 2)
            nc.vector.quantize_mx(out=p_codes[c][:, 512 * G:512 * G + 512].bitcast(FP8X4), scales=p_scales[c][4 * G:P, :], in_=p_grouped[s][:])

        def stage2_matmuls(s, n):
            c, r = divmod(s, 4)
            acc = psum.tile([P, 512], F32, name="m2", tag="m2")
            for G in range(4):
                a_codes, a_sc = a_operand(G, n)
                lo = 512 * G + P * r
                nc.tensor.matmul_mx(
                    out=acc[:], lhsT=p_codes[c][:, lo:lo + P].bitcast(FP8X4), lhsT_scale=p_scales[c][4 * G:P, P * r:P * r + P],
                    rhs=a_codes.bitcast(FP8X4), rhs_scale=a_sc[4 * G:P, :], start=(G == 0), stop=(G == 3),
                )
            acc2[(s, n)] = acc

        def stage2_store(s, n):
            c, r = divmod(s, 4)
            rows, r0, m, out = chunk_info(c)
            staged = sb_tile([P, 512], F32, "ob", OUT_BUFS)
            nc.scalar.copy(out=staged[:], in_=acc2[(s, n)][:])
            nc.sync.dma_start(out=out[r0 + P * r:r0 + P * r + P, 512 * n:512 * n + 512], in_=staged[:])

        load_next_pair()
        load_next_pair()
        for n in range(ROW_BUFS):
            load_next_rows()

        for slot in range(-8, 4 * (STEPS1 + LAG)):
            s, j = divmod(slot, 4)
            if slot in EARLY_PAIR_SLOTS:
                load_next_pair()
            for job in tensor_jobs.get(slot, []):
                tensor_sort(job)
            for job in tensor_jobs.get(slot - 2, []):
                quantize(job)
            for job in tensor_jobs.get(slot - 1, []):
                tensor_transpose(job)
            for job in tensor_jobs.get(slot - 1, []):
                tensor_copy_out(job)

            if 0 <= s < STEPS1:
                stage1_matmuls(s, j)
            if 0 <= s - LAG < STEPS1:
                stage2_matmuls(s - LAG, j)
            if 0 <= s < STEPS1:
                stage1_bias_round(s, j)
            if 0 <= s - LAG < STEPS1:
                stage2_store(s - LAG, j)

            x_job, w_job = x_jobs.get(s), w_es_jobs.get(s)
            if j == 0:
                if x_job:
                    vector_transpose(x_job)
                if 0 <= s - 1 < STEPS1:
                    p_interleave(s - 1)
            if j == 1:
                if x_job:
                    vector_interleave(x_job)
                if 0 <= s - 1 < STEPS1:
                    p_quantize(s - 1)
            if j == 2:
                if w_job:
                    vector_transpose(w_job)
                if x_job:
                    quantize(x_job)
            if j == 3 and w_job:
                vector_interleave(w_job)
                quantize(w_job)

            next_x, next_w = x_jobs.get(s + 1), w_es_jobs.get(s + 1)
            if j < 2 and next_x:
                vector_sort(next_x, j)
            if j >= 2 and next_w:
                vector_sort(next_w, j - 2)
                if j == 3:
                    load_next_rows()
            if j == 2 and s >= 4 and s % 2 == 0:
                load_next_pair()
